import numpy as np
import ml_dtypes


def mxq(x, axis, fmt="e4m3"):
    dtype, down = {"e4m3": (ml_dtypes.float8_e4m3fn, 7), "e5m2": (ml_dtypes.float8_e5m2, 14)}[fmt]
    v = np.moveaxis(np.asarray(x, np.float32).astype(ml_dtypes.bfloat16).astype(np.float64), axis, -1)
    blocks = v.reshape(v.shape[:-1] + (-1, 32))
    amax = np.abs(blocks).max(-1, keepdims=True)
    byte = np.maximum(np.where(amax > 0, np.frexp(amax)[1] - 1 + 127, 0) - down, 1)
    scale = np.exp2(byte - 127.0)
    codes = (blocks / scale).astype(np.float32).astype(dtype).astype(np.float64)
    return np.moveaxis((codes * scale).reshape(v.shape), -1, axis)


WIDE = False


def mx_kscale(k):
    if not WIDE:
        return np.ones(k)
    levels = np.array([10, -10, 5, -5, 0])
    if k % 512:
        return np.exp2(np.random.permutation(np.resize(levels, k // 32))).repeat(32)
    a = np.empty((k // 512, 16))
    for p in range(k // 512):
        a[p, :8] = np.random.permutation(np.resize(levels, 8))
        for g in range(8):
            far = levels[np.abs(levels - a[p, g]) >= 10]
            a[p, g + 8] = far[np.random.randint(len(far))]
    return np.exp2(a.ravel()).repeat(32)


BF16 = ml_dtypes.bfloat16


def bf(x):
    return np.asarray(x, np.float32).astype(BF16)


def f64(x):
    return np.asarray(x).astype(np.float64)


B, S, H, E, D, TRAIN_LEN = 1, 1024, 1024, 1536, 128, 512


def silu(v):
    return v / (1.0 + np.exp(-v))


def apply_rotary(x, sin, cos):
    x1, x2 = x[..., 0::2], x[..., 1::2]
    return np.concatenate([x1 * cos - x2 * sin, x1 * sin + x2 * cos], axis=-1)


def setup_inputs():
    s = mx_kscale(H)
    pos = np.arange(S)[:, None]
    inv = np.exp(-np.arange(0, D, 2) / D * np.log(10000.0))
    ang = pos * inv[None, :]
    return {"hidden_states": bf(np.random.standard_normal((B, S, H)) * s),
            "sin": bf(np.sin(ang)[None]),
            "cos": bf(np.cos(ang)[None]),
            "W_i": bf(np.random.standard_normal((H, 2 * E + D)) / np.sqrt(H) / s[:, None]),
            "q_scale": bf(1.0 + 0.1 * np.random.standard_normal(D)),
            "k_scale": bf(1.0 + 0.1 * np.random.standard_normal(D))}


def reference(hidden_states, sin, cos, W_i, q_scale, k_scale):
    x = silu(mxq(f64(hidden_states), 2, "e4m3") @ mxq(f64(W_i), 0, "e4m3"))
    u, v, qk = np.split(x, [E, 2 * E], axis=-1)
    sn, cs = f64(sin), f64(cos)
    q = apply_rotary(qk * f64(q_scale), sn, cs)
    k = apply_rotary(qk * f64(k_scale), sn, cs)
    return u, v, q, k

from contextlib import ExitStack

import concourse.mybir as mybir
from concourse.masks import make_identity

F32 = mybir.dt.float32
BF16 = mybir.dt.bfloat16
U32 = mybir.dt.uint32
U8 = mybir.dt.uint8
FP8X4 = mybir.dt.float8_e4m3fn_x4
SILU = mybir.ActivationFunctionType.Silu
MULT = mybir.AluOpType.mult
ADD = mybir.AluOpType.add
SUB = mybir.AluOpType.subtract

P = 128
NT = 8
E = 1536
D = 128
CH = 512
VW = E + D

FLOPS = 2 * 1024 * 1024 * 3200


def tile_gatedattentionunit_pa_kernel(
    tc, hidden_states, sin, cos, W_i, q_scale, k_scale, out_0, out_1, out_2, out_3
):
    nc = tc.nc
    x_dram = hidden_states.flatten_outer_dims().rearrange("(p i) k -> p i k", i=NT)
    cos_dram = cos.flatten_outer_dims().rearrange("(p i) j -> p i j", i=NT)
    sin_dram = sin.flatten_outer_dims().rearrange("(p i) j -> p i j", i=NT)
    w_by_g = W_i.rearrange("(g p t) n -> g p t n", g=2, t=4)
    w_by_gh = W_i.rearrange("(g p h e) n -> g h p e n", g=2, h=2, e=2)
    u_dram = out_0.flatten_outer_dims().rearrange("(p j r) c -> j p r c", j=NT // 2, r=2)
    v_dram = out_1.flatten_outer_dims().rearrange("(p j r) c -> j p r c", j=NT // 2, r=2)
    q_dram = out_2.flatten_outer_dims().rearrange("(p i) c -> p i c", i=NT)
    k_dram = out_3.flatten_outer_dims().rearrange("(p i) c -> p i c", i=NT)

    with ExitStack() as ctx:
        keep = ctx.enter_context(tc.tile_pool(name="keep", bufs=1))
        xgp = ctx.enter_context(tc.tile_pool(name="xgp", bufs=3))
        wgp = ctx.enter_context(tc.tile_pool(name="wgp", bufs=3))
        stage = ctx.enter_context(tc.tile_pool(name="stage", bufs=6))
        rot = ctx.enter_context(tc.tile_pool(name="rot", bufs=1))
        psum = ctx.enter_context(tc.psum_pool(name="psum", bufs=8))
        ctx.enter_context(tc.manual_schedule())

        ident = keep.tile([P, P], F32, name="ident")
        ones = keep.tile([P, P], BF16, name="ones")
        gsrc = keep.tile([P, 2 * D], BF16, name="gsrc")
        gains = keep.tile([P, 2, D], F32, name="gains")
        tab = keep.tile([P, 2, NT, D // 2], BF16, name="tab")
        x_codes = keep.tile([P, NT, 2, P], U32, name="x_codes", align_bytes=64)
        x_scales = keep.tile([P, NT, 2, P], U8, name="x_scales", align_bytes=64)
        w_codes = keep.tile([P, 2, 2 * E], U32, name="w_codes", align_bytes=64)
        w_scales = keep.tile([P, 2, 2 * E], U8, name="w_scales", align_bytes=64)
        wq_codes = keep.tile([P, 2, D], U32, name="wq_codes", align_bytes=64)
        wq_scales = keep.tile([P, 2, D], U8, name="wq_scales", align_bytes=64)
        wq_grp = keep.tile([P, 2, D, 4], BF16, name="wq_grp", align_bytes=64)
        w0_raw = keep.tile([P, 4, 2, CH], BF16, name="w0_raw")
        w12_raw = keep.tile([P, 4, 2, 2 * CH], BF16, name="w12_raw")
        wv_raw = keep.tile([P, 4, 2, VW], BF16, name="wv_raw")
        z = keep.tile([P, NT, D], F32, name="z")
        x_raw = [keep.tile([P, 2, 1024], BF16, name="x_raw%d" % d) for d in range(4)]

        make_identity(nc, ident[:])
        nc.gpsimd.memset(ones[:], 1.0)
        nc.gpsimd.memset(gsrc[:], 0.0)

        for g in range(2):
            nc.sync.dma_start(
                out=w0_raw[:, 2 * g : 2 * g + 2, :, :].rearrange("p h e n -> p (h e) n"),
                in_=w_by_g[g, :, :, 0:CH],
            )
        for d in range(2):
            nc.sync.dma_start(out=x_raw[d][:], in_=x_dram[:, 2 * d : 2 * d + 2, :])
        for a in range(4):
            nc.sync.dma_start(out=w12_raw[:, a, :, :], in_=w_by_gh[a // 2, a % 2, :, :, CH:E])
        for d in range(2, 4):
            nc.sync.dma_start(out=x_raw[d][:], in_=x_dram[:, 2 * d : 2 * d + 2, :])
        for a in range(4):
            nc.sync.dma_start(out=wv_raw[:, a, :, :], in_=w_by_gh[a // 2, a % 2, :, :, E : E + VW])
        nc.sync.dma_start(out=tab[:, 0, :, :], in_=cos_dram)
        nc.sync.dma_start(out=tab[:, 1, :, :], in_=sin_dram)
        nc.sync.dma_start(out=gsrc[0:1, 0:D], in_=q_scale.rearrange("(o d) -> o d", o=1))
        nc.sync.dma_start(out=gsrc[0:1, D : 2 * D], in_=k_scale.rearrange("(o d) -> o d", o=1))

        def w_src(c, g):
            if c == 0:
                raw, lo = w0_raw, 0
            elif c < 3:
                raw, lo = w12_raw, (c - 1) * CH
            else:
                raw, lo = wv_raw, (c - 3) * CH
            return raw[:, 2 * g : 2 * g + 2, :, lo : lo + CH].rearrange("p u e n -> p (u e) n")

        grouped = {}

        def regroup(job):
            if job == "qk":
                src = wv_raw[:, :, :, E : E + D].rearrange("p (g u) e n -> p g (u e) n", g=2)
                nc.vector.tensor_copy(out=wq_grp[:], in_=src.rearrange("p g t n -> p g n t"))
                return
            c, g = job
            t = wgp.tile([P, CH, 4], BF16, name="wgrp%d_%d" % (c, g), tag="wgrp", align_bytes=64)
            nc.vector.tensor_copy(
                out=t[:].rearrange("p (n i) t -> p n t i", i=4),
                in_=w_src(c, g).rearrange("p t (n i) -> p n t i", i=4),
            )
            grouped[job] = t

        def quantise(job):
            if job == "qk":
                nc.vector.quantize_mx(
                    out=wq_codes[:].rearrange("p g n -> p (g n)").bitcast(FP8X4),
                    scales=wq_scales[:].rearrange("p g n -> p (g n)"),
                    in_=wq_grp[:].rearrange("p g n t -> p (g n t)"),
                )
                return
            c, g = job
            cols = slice(c * CH, (c + 1) * CH)
            nc.vector.quantize_mx(
                out=w_codes[:, g, cols].bitcast(FP8X4),
                scales=w_scales[:, g, cols],
                in_=grouped[job][:].rearrange("p n t -> p (n t)"),
            )

        xg = {}

        def x_transpose(i):
            d, r = divmod(i, 2)
            if r == 0:
                xg[d] = xgp.tile([P, 2, 2, P, 4], BF16, name="xg%d" % d, tag="xg", align_bytes=64)
            xt = psum.tile([P, 4, P], F32, name="xt%d" % i, tag="bank")
            words = x_raw[d][:, r, :].bitcast(F32)
            for g in range(2):
                for h in range(2):
                    every_2nd = words[:, 2 * P * g + h : 2 * P * (g + 1) : 2]
                    nc.tensor.transpose(xt[:, 2 * g + h, :], every_2nd, ident[:])
            nc.scalar.copy(
                out=xg[d][:, r, :, :, :].bitcast(F32),
                in_=xt[:].rearrange("p (g u) r -> p g r u", u=2),
            )

        def x_quantise(d):
            nc.vector.quantize_mx(
                out=x_codes[:, 2 * d : 2 * d + 2].rearrange("p i g r -> p (i g r)").bitcast(FP8X4),
                scales=x_scales[:, 2 * d : 2 * d + 2].rearrange("p i g r -> p (i g r)"),
                in_=xg[d][:].rearrange("p i g r t -> p (i g r t)"),
            )

        def mx(acc, i, codes, scales):
            for g in range(2):
                nc.tensor.matmul_mx(
                    out=acc,
                    lhsT=x_codes[:, i, g, :].bitcast(FP8X4),
                    lhsT_scale=x_scales[:, i, g, :],
                    rhs=codes(g).bitcast(FP8X4),
                    rhs_scale=scales(g),
                    start=(g == 0),
                    stop=(g == 1),
                )

        def mx_chunk(i, c, pair):
            cols = slice(c * CH, (c + 1) * CH)
            acc = psum.tile([P, CH], F32, name="acc%d_%d" % (c, i), tag="bank")
            mx(acc[:], i, lambda g: w_codes[:, g, cols], lambda g: w_scales[:, g, cols])
            lo = (c % 3) * CH
            nc.scalar.activation(out=pair[:, i % 2, lo : lo + CH], in_=acc[:], func=SILU)

        def pair_tile(name):
            return stage.tile([P, 2, E], F32, name=name, tag="stage")

        regroup((0, 0))
        regroup((0, 1))
        quantise((0, 0))
        x_transpose(0)
        x_transpose(1)
        x_quantise(0)
        quantise((0, 1))
        x_transpose(2)
        x_transpose(3)
        x_quantise(1)

        def store_pair(dram, j, pair):
            nc.sync.dma_start(out=dram[j, :, :, :], in_=pair[:])

        u_sb = [pair_tile("u_sb%d" % j) for j in range(NT // 2)]
        for i in range(4):
            mx_chunk(i, 0, u_sb[i // 2])
        regroup((1, 0))
        regroup((2, 0))
        regroup((1, 1))
        quantise((1, 0))
        quantise((1, 1))
        regroup((2, 1))
        quantise((2, 0))
        quantise((2, 1))
        x_transpose(4)
        x_transpose(5)
        x_quantise(2)
        for i in range(4):
            mx_chunk(i, 1, u_sb[i // 2])
        for i in range(4):
            mx_chunk(i, 2, u_sb[i // 2])
            if i % 2 == 1:
                store_pair(u_dram, i // 2, u_sb[i // 2])
        x_transpose(6)
        x_transpose(7)

        regroup((3, 0))
        regroup((4, 0))
        quantise((3, 0))
        x_quantise(3)
        regroup((5, 0))
        quantise((4, 0))
        regroup("qk")
        quantise((5, 0))
        regroup((3, 1))
        quantise("qk")
        regroup((4, 1))
        quantise((3, 1))
        regroup((5, 1))
        quantise((4, 1))
        quantise((5, 1))

        for j in (2, 3):
            for i in (2 * j, 2 * j + 1):
                for c in range(3):
                    mx_chunk(i, c, u_sb[j])
            store_pair(u_dram, j, u_sb[j])

        gps = psum.tile([P, CH], F32, name="gps", tag="bank")
        nc.tensor.matmul(out=gps[:, 0 : 2 * D], lhsT=ones[:], rhs=gsrc[:], start=True, stop=True)
        nc.scalar.copy(out=gains[:].rearrange("p s d -> p (s d)"), in_=gps[:, 0 : 2 * D])
        for h in range(2):
            zb = psum.tile([P, 4, D], F32, name="zb%d" % h, tag="bank")
            for r in range(4):
                mx(zb[:, r, :], 4 * h + r, lambda g: wq_codes[:, g, :], lambda g: wq_scales[:, g, :])
            nc.scalar.activation(out=z[:, 4 * h : 4 * h + 4, :], in_=zb[:], func=SILU)

        def rotate(s, dram):
            y = rot.tile([P, NT, D], F32, name="y%d" % s, tag="y")
            m_cos = rot.tile([P, NT, 2, D // 2], F32, name="mc%d" % s, tag="mc", bufs=2)
            m_sin = rot.tile([P, NT, 2, D // 2], F32, name="ms%d" % s, tag="ms")
            nc.vector.tensor_tensor(
                out=y[:], in0=z[:], in1=gains[:, s, :].unsqueeze(1).to_broadcast([P, NT, D]), op=MULT
            )
            pairs = y[:].rearrange("p i (j e) -> p i e j", e=2)
            shape = [P, NT, 2, D // 2]
            nc.vector.tensor_tensor(
                out=m_cos[:], in0=pairs, in1=tab[:, 0, :, :].unsqueeze(2).to_broadcast(shape), op=MULT
            )
            nc.vector.tensor_tensor(
                out=m_sin[:], in0=pairs, in1=tab[:, 1, :, :].unsqueeze(2).to_broadcast(shape), op=MULT
            )
            nc.vector.tensor_tensor(out=m_cos[:, :, 0, :], in0=m_cos[:, :, 0, :], in1=m_sin[:, :, 1, :], op=SUB)
            nc.vector.tensor_tensor(out=m_cos[:, :, 1, :], in0=m_cos[:, :, 1, :], in1=m_sin[:, :, 0, :], op=ADD)
            nc.sync.dma_start(out=dram, in_=m_cos[:].rearrange("p i h j -> p i (h j)"))

        def v_tile(i, pair):
            for c in range(3, 6):
                mx_chunk(i, c, pair)

        v01 = pair_tile("v_sb0")
        v_tile(0, v01)
        v_tile(1, v01)
        store_pair(v_dram, 0, v01)
        rotate(0, q_dram)
        v23 = pair_tile("v_sb1")
        v_tile(2, v23)
        v_tile(3, v23)
        store_pair(v_dram, 1, v23)
        v45 = pair_tile("v_sb2")
        v_tile(4, v45)
        v_tile(5, v45)
        store_pair(v_dram, 2, v45)
        rotate(1, k_dram)
        v67 = pair_tile("v_sb3")
        v_tile(6, v67)
        nc.sync.dma_start(out=v_dram[3, :, 0, :], in_=v67[:, 0, :])
        v_tile(7, v67)
        nc.sync.dma_start(out=v_dram[3, :, 1, :], in_=v67[:, 1, :])
